import numpy as np
import ml_dtypes


def mxq(x, axis, fmt="e4m3"):
    dtype, down = {"e4m3": (ml_dtypes.float8_e4m3fn, 7), "e5m2": (ml_dtypes.float8_e5m2, 14)}[fmt]
    v = np.moveaxis(np.asarray(x, np.float32).astype(ml_dtypes.bfloat16).astype(np.float64), axis, -1)
    blocks = v.reshape(v.shape[:-1] + (-1, 32))
    amax = np.abs(blocks).max(-1, keepdims=True)
    byte = np.maximum(np.where(amax > 0, np.frexp(amax)[1] - 1 + 127, 0) - down, 1)
    scale = np.exp2(byte - 127.0)
    codes = (blocks / scale).astype(np.float32).astype(dtype).astype(np.float64)
    return np.moveaxis((codes * scale).reshape(v.shape), -1, axis)


WIDE = False


def mx_kscale(k):
    if not WIDE:
        return np.ones(k)
    levels = np.array([10, -10, 5, -5, 0])
    if k % 512:
        return np.exp2(np.random.permutation(np.resize(levels, k // 32))).repeat(32)
    a = np.empty((k // 512, 16))
    for p in range(k // 512):
        a[p, :8] = np.random.permutation(np.resize(levels, 8))
        for g in range(8):
            far = levels[np.abs(levels - a[p, g]) >= 10]
            a[p, g + 8] = far[np.random.randint(len(far))]
    return np.exp2(a.ravel()).repeat(32)


BF16 = ml_dtypes.bfloat16


def bf(x):
    return np.asarray(x, np.float32).astype(BF16)


def f64(x):
    return np.asarray(x).astype(np.float64)


B, D_IN, D_HID, SHARE = 1024, 512, 256, 2
NUM_GATE = 4 + SHARE


def sigmoid(v):
    return 1.0 / (1.0 + np.exp(-v))


def setup_inputs():
    s = mx_kscale(D_IN)
    n = np.random.standard_normal
    return {
        "input": bf(n((B, D_IN)) * s),
        "h_minors": bf(n((B, D_HID))),
        "c_minors": bf(n((B, D_HID))),
        "s_minors": bf(n((SHARE, B, D_HID))),
        "mask": bf(np.random.uniform(0.5, 1.5, B)),
        "weight_ih": bf(n((NUM_GATE * D_HID, D_IN)) * 0.7 / np.sqrt(D_IN) / s),
        "weight_hh": bf(n((4 * D_HID, D_HID)) * 0.7 / np.sqrt(D_HID)),
        "weight_sh": bf(n((SHARE * D_HID, D_HID)) * 0.7 / np.sqrt(D_HID)),
        "bias_ih": bf(n(NUM_GATE * D_HID) * 0.3),
        "bias_hh": bf(n(4 * D_HID) * 0.3),
        "bias_sh": bf(n(SHARE * D_HID) * 0.3),
        "idx": 0,
    }


def reference(input, h_minors, c_minors, s_minors, mask, weight_ih, weight_hh, weight_sh, bias_ih, bias_hh, bias_sh, idx):
    H = weight_hh.shape[1]
    share = weight_sh.shape[0] // H
    m = f64(mask)[:, None]
    tmp = (mxq(f64(input), 1, "e4m3") @ mxq(f64(weight_ih), 1, "e4m3").T) + f64(bias_ih)
    tmp2 = f64(h_minors) @ f64(weight_hh).T + f64(bias_hh)
    tmp3 = f64(s_minors)[idx] @ f64(weight_sh).T + f64(bias_sh)
    tmp_in, tmp_s = tmp[:, :4 * H], tmp[:, 4 * H:]
    z = tmp_in + tmp2
    ifo = sigmoid(z[:, :3 * H])
    i, f, o = ifo[:, :H], ifo[:, H:2 * H], ifo[:, 2 * H:]
    c_hat = z[:, 3 * H:]
    b = sigmoid(tmp_s + tmp3)
    c_t = (f * f64(c_minors) + i * np.tanh(c_hat)) * m
    tc = np.tanh(c_t) * m
    h = o * tc
    s = b.reshape(-1, share, H) * tc[:, None, :]
    s = np.moveaxis(s, 1, 0)
    return (h, c_t, s[0], s[1])

@@ -1,0 +1,373 @@
+from contextlib import ExitStack
+
+import concourse.mybir as mybir
+from concourse.masks import make_identity
+
+FP8X4 = mybir.dt.float8_e4m3fn_x4
+BF16 = mybir.dt.bfloat16
+F32 = mybir.dt.float32
+U32 = mybir.dt.uint32
+U8 = mybir.dt.uint8
+ACT = mybir.ActivationFunctionType
+ALU = mybir.AluOpType
+
+P = 128
+PACK = 4
+BATCH = 1024
+D_IN = 512
+HID = 256
+N_TILES = BATCH // P
+WORDS = D_IN // 2
+K_CHUNKS = HID // P
+N_GATES = 6
+N_PAIRS = N_GATES // 2
+N_RECURRENT = 4
+PAIR_COLS = 2 * HID
+GATE_TILES = N_GATES * HID // P
+PSUM_BANKS = 8
+SIDE = 4
+HALF_COLS = SIDE * P
+N_HALVES = N_TILES // SIDE
+MX_AT = 3
+
+assert SIDE == 2 * K_CHUNKS
+
+FLOPS = 2 * BATCH * (D_IN * N_GATES * HID + HID * N_GATES * HID)
+BYTES = (
+    2 * (BATCH * D_IN + 3 * BATCH * HID + BATCH)
+    + 2 * (N_GATES * HID * (D_IN + HID) + 2 * N_GATES * HID)
+    + 4 * 4 * BATCH * HID
+)
+
+
+def tile_share_lstm_cell_kernel(
+    tc,
+    x,
+    h_minors,
+    c_minors,
+    s_minors,
+    mask,
+    weight_ih,
+    weight_hh,
+    weight_sh,
+    bias_ih,
+    bias_hh,
+    bias_sh,
+    idx,
+    out_h,
+    out_c,
+    out_s0,
+    out_s1,
+):
+    nc = tc.nc
+
+    def by_batch_tile(dram):
+        return dram.rearrange("(p t) n -> p t n", t=N_TILES)
+
+    with ExitStack() as ctx:
+        keep = ctx.enter_context(tc.tile_pool(name="keep", bufs=1))
+        stage = ctx.enter_context(tc.tile_pool(name="stage", bufs=3))
+        mx_pool = ctx.enter_context(tc.tile_pool(name="mx_pool", bufs=2))
+        psum = ctx.enter_context(tc.psum_pool(name="psum", bufs=PSUM_BANKS))
+        ctx.enter_context(tc.manual_schedule())
+
+        bias_rows = keep.tile([P, P], BF16)
+        nc.gpsimd.memset(bias_rows[:], 0.0)
+        ident_f32 = keep.tile([P, P], F32)
+        make_identity(nc, ident_f32[:])
+        ident_bf16 = keep.tile([P, P], BF16)
+        nc.vector.tensor_copy(out=ident_bf16[:], in_=ident_f32[:])
+
+        x_sb = keep.tile([P, N_TILES * D_IN], BF16)
+        h_sb = keep.tile([P, N_TILES * HID], BF16)
+        s_sb = keep.tile([P, N_TILES * HID], BF16)
+        c_sb = keep.tile([P, N_TILES, HID], BF16)
+        w_in_sb = keep.tile([P, N_GATES * 2 * D_IN], BF16)
+        w_rec_sb = keep.tile([P, N_GATES * 2 * HID], BF16)
+        mask_sb = keep.tile([P, N_TILES], BF16)
+
+        def load_batch(tile_sb, dram, first, count):
+            view = tile_sb[:].rearrange("p (t n) -> p t n", t=N_TILES)
+            nc.sync.dma_start(
+                out=view[:, first : first + count, :],
+                in_=by_batch_tile(dram)[:, first : first + count, :],
+            )
+
+        def load_gate(tile_sb, rows, gate):
+            width = rows.shape[1]
+            nc.sync.dma_start(
+                out=tile_sb[:, gate * 2 * width : (gate + 1) * 2 * width].rearrange(
+                    "p (r n) -> p r n", r=2
+                ),
+                in_=rows.rearrange("(r p) n -> p r n", p=P),
+            )
+
+        def load_in_weights(gate):
+            load_gate(w_in_sb, weight_ih[gate * HID : (gate + 1) * HID, :], gate)
+
+        def load_recurrent_weights(gate):
+            if gate < N_RECURRENT:
+                load_gate(w_rec_sb, weight_hh[gate * HID : (gate + 1) * HID, :], gate)
+            else:
+                share = gate - N_RECURRENT
+                load_gate(w_rec_sb, weight_sh[share * HID : (share + 1) * HID, :], gate)
+
+        def as_rows(vector):
+            return vector.rearrange("(r n) -> r n", n=P)
+
+        rec_rows = N_RECURRENT * HID // P
+        warm = keep.tile([P, 1], F32)
+        nc.vector.memset(warm[:], 0.0)
+        nc.scalar.activation(out=warm[:], in_=warm[:], func=ACT.Sigmoid)
+        load_in_weights(0)
+        load_batch(x_sb, x, 0, 2)
+        load_batch(x_sb, x, 2, 2)
+        load_in_weights(1)
+        nc.sync.dma_start(out=bias_rows[0:GATE_TILES, :], in_=as_rows(bias_ih))
+        nc.sync.dma_start(out=bias_rows[GATE_TILES : GATE_TILES + rec_rows, :], in_=as_rows(bias_hh))
+        nc.sync.dma_start(out=bias_rows[GATE_TILES + rec_rows : 2 * GATE_TILES, :], in_=as_rows(bias_sh))
+        load_recurrent_weights(0)
+        load_recurrent_weights(1)
+        load_batch(h_sb, h_minors, 0, SIDE)
+        load_batch(x_sb, x, SIDE, SIDE)
+        load_in_weights(2)
+        load_in_weights(3)
+        load_batch(h_sb, h_minors, SIDE, SIDE)
+        load_recurrent_weights(2)
+        load_recurrent_weights(3)
+        nc.sync.dma_start(out=mask_sb[:], in_=mask.rearrange("(p t) -> p t", t=N_TILES))
+        nc.sync.dma_start(out=c_sb[:], in_=by_batch_tile(c_minors))
+        load_in_weights(4)
+        load_in_weights(5)
+        load_recurrent_weights(4)
+        load_recurrent_weights(5)
+        load_batch(s_sb, s_minors[idx, :, :], 0, N_TILES)
+
+        bias_col = keep.tile([P, GATE_TILES], F32)
+
+        def turn_biases():
+            bias_turned = psum.tile([P, P], BF16, tag="bank")
+            nc.tensor.transpose(bias_turned[:], bias_rows[:], ident_bf16[:])
+            bias_parts = keep.tile([P, 2 * GATE_TILES], F32)
+            nc.vector.tensor_copy(out=bias_parts[:], in_=bias_turned[:, 0 : 2 * GATE_TILES])
+            nc.vector.tensor_tensor(
+                out=bias_col[:], in0=bias_parts[:, 0:GATE_TILES], in1=bias_parts[:, GATE_TILES:], op=ALU.add
+            )
+
+        mask_f32 = keep.tile([P, N_TILES], F32)
+        nc.gpsimd.tensor_copy(out=mask_f32[:], in_=mask_sb[:])
+
+        x_codes = keep.tile([P, N_TILES * P], U32, align_bytes=64)
+        x_scales = keep.tile([P, N_TILES * P], U8, align_bytes=64)
+        w_codes = keep.tile([P, N_GATES * HID], U32, align_bytes=64)
+        w_scales = keep.tile([P, N_GATES * HID], U8, align_bytes=64)
+        h_T_words = keep.tile([P, N_TILES * P], F32)
+        s_T_words = keep.tile([P, N_TILES * P], F32)
+        w_rec_T_words = keep.tile([P, N_PAIRS * PAIR_COLS], F32)
+        h_T = h_T_words[:].bitcast(BF16).rearrange("p (t b e) -> p t b e", t=N_TILES, e=2)
+        s_T = s_T_words[:].bitcast(BF16).rearrange("p (t b e) -> p t b e", t=N_TILES, e=2)
+        w_rec_T = w_rec_T_words[:].bitcast(BF16).rearrange("p (g n e) -> p g n e", g=N_PAIRS, e=2)
+
+        def turn_two_blocks(source_sb, first_block, copy_out):
+            words = source_sb[:].bitcast(F32)
+            turned = psum.tile([P, 2, 2, P], F32, tag="bank")
+            for j in range(2):
+                for u in range(2):
+                    first = (first_block + j) * WORDS + u
+                    last = (first_block + j + 1) * WORDS
+                    nc.tensor.transpose(turned[:, j, u, :], words[:, first:last:2], ident_f32[:])
+            grouped = stage.tile([P, 2 * P * PACK], BF16, align_bytes=64)
+            copy_out(
+                out=grouped[:].bitcast(F32).rearrange("p (j r u) -> p j r u", j=2, u=2),
+                in_=turned[:].rearrange("p j u r -> p j r u"),
+            )
+            return grouped
+
+        def quantise_two_blocks(grouped, codes, scales, first_block):
+            cols = slice(first_block * P, (first_block + 2) * P)
+            nc.vector.quantize_mx(
+                out=codes[:, cols].bitcast(FP8X4), scales=scales[:, cols], in_=grouped[:]
+            )
+
+        def turn_four_blocks(source_sb, dest_words, first_block, copy_out):
+            words = source_sb[:].bitcast(F32)
+            turned = psum.tile([P, SIDE * P], F32, tag="bank")
+            for i in range(SIDE):
+                cols = slice((first_block + i) * P, (first_block + i + 1) * P)
+                nc.tensor.transpose(turned[:, i * P : (i + 1) * P], words[:, cols], ident_f32[:])
+            copy_out(out=dest_words[:, first_block * P : (first_block + SIDE) * P], in_=turned[:])
+
+        def mx_products(pair, half):
+            mx_T = mx_pool.tile([P, SIDE, HALF_COLS], F32)
+            batch = slice(half * HALF_COLS, (half + 1) * HALF_COLS)
+            banks = []
+            for j in range(SIDE):
+                gate_tile = SIDE * pair + j
+                rows = slice(gate_tile * P, (gate_tile + 1) * P)
+                acc_mx = psum.tile([P, HALF_COLS], F32, tag="bank")
+                nc.tensor.matmul_mx(
+                    out=acc_mx[:],
+                    lhsT=w_codes[:, rows].bitcast(FP8X4),
+                    lhsT_scale=w_scales[:, rows],
+                    rhs=x_codes[:, batch].bitcast(FP8X4),
+                    rhs_scale=x_scales[:, batch],
+                    start=True,
+                    stop=True,
+                )
+                banks.append(acc_mx)
+            for j in range(SIDE):
+                bias = bias_col[:, SIDE * pair + j : SIDE * pair + j + 1]
+                if j % 2 == 0:
+                    nc.scalar.activation(out=mx_T[:, j, :], in_=banks[j][:], func=ACT.Identity, bias=bias)
+                else:
+                    nc.vector.tensor_scalar_add(out=mx_T[:, j, :], in0=banks[j][:], scalar1=bias)
+            return mx_T
+
+        steps = [
+            (pair, half * SIDE + q)
+            for pair in range(N_PAIRS)
+            for half in range(N_HALVES)
+            for q in range(SIDE)
+        ]
+        gates = keep.tile([P, N_PAIRS, N_TILES, PAIR_COLS], F32)
+        mx_T_of = {}
+        pre_of = {}
+
+        def plain_pass(pair, t, c):
+            if c == 0:
+                bank = psum.tile([P, PAIR_COLS], F32, tag="bank")
+                pre_of[(pair, t)] = bank
+            state_T = h_T if 2 * pair < N_RECURRENT else s_T
+            nc.tensor.matmul(
+                out=pre_of[(pair, t)][:],
+                lhsT=state_T[:, t, :, c],
+                rhs=w_rec_T[:, pair, :, c],
+                start=(c == 0),
+                stop=False,
+            )
+
+        def add_mx_product(pair, t, j):
+            q = t % SIDE
+            nc.tensor.matmul(
+                out=pre_of[(pair, t)][:, j * P : (j + 1) * P],
+                lhsT=mx_T_of[(pair, t // SIDE)][:, j, q * P : (q + 1) * P],
+                rhs=ident_f32[:],
+                is_transpose=True,
+                start=False,
+                stop=(j == SIDE - 1),
+            )
+
+        def activations(pair, t):
+            pre = pre_of[(pair, t)]
+            if pair == 1:
+                nc.scalar.activation(out=gates[:, pair, t, 0:HID], in_=pre[:, 0:HID], func=ACT.Sigmoid)
+                nc.scalar.activation(out=gates[:, pair, t, HID:], in_=pre[:, HID:], func=ACT.Tanh)
+            else:
+                nc.scalar.activation(out=gates[:, pair, t, :], in_=pre[:], func=ACT.Sigmoid)
+
+        kept = keep.tile([P, N_TILES, HID], F32)
+        cell = keep.tile([P, N_TILES, HID], F32)
+        squashed = keep.tile([P, N_TILES, HID], F32)
+        h_res = keep.tile([P, N_TILES, HID], F32)
+        c_res = keep.tile([P, N_TILES, HID], F32)
+        s_res = keep.tile([P, 2, N_TILES, HID], F32)
+
+        def store(dram, result, t):
+            nc.sync.dma_start(out=by_batch_tile(dram)[:, t, :], in_=result[:, t, :])
+
+        def times_masked_tanh(out, gate, t):
+            nc.vector.scalar_tensor_tensor(
+                out=out,
+                in0=squashed[:, t, :],
+                scalar=mask_f32[:, t : t + 1],
+                in1=gate,
+                op0=ALU.mult,
+                op1=ALU.mult,
+            )
+
+        def products(pair, t):
+            if pair == 0:
+                nc.vector.tensor_tensor(
+                    out=kept[:, t, :], in0=gates[:, 0, t, HID:], in1=c_sb[:, t, :], op=ALU.mult
+                )
+            elif pair == 1:
+                in_term = stage.tile([P, HID], F32)
+                nc.vector.tensor_tensor(
+                    out=in_term[:], in0=gates[:, 0, t, 0:HID], in1=gates[:, 1, t, HID:], op=ALU.mult
+                )
+                nc.vector.tensor_tensor(out=cell[:, t, :], in0=in_term[:], in1=kept[:, t, :], op=ALU.add)
+            else:
+                for share in range(2):
+                    times_masked_tanh(s_res[:, share, t, :], gates[:, 2, t, share * HID : (share + 1) * HID], t)
+                store(out_s0, s_res[:, 0, :, :], t)
+                store(out_s1, s_res[:, 1, :, :], t)
+
+        def new_cell(pair, t):
+            if pair == 1:
+                m = mask_f32[:, t : t + 1]
+                nc.scalar.activation(out=squashed[:, t, :], in_=cell[:, t, :], func=ACT.Tanh, scale=m)
+                nc.vector.tensor_scalar_mul(out=c_res[:, t, :], in0=cell[:, t, :], scalar1=m)
+                store(out_c, c_res, t)
+
+        def new_hidden(pair, t):
+            if pair == 1:
+                times_masked_tanh(h_res[:, t, :], gates[:, 1, t, 0:HID], t)
+                store(out_h, h_res, t)
+
+        first_w = turn_two_blocks(w_in_sb, 0, nc.vector.tensor_copy)
+        first_x = turn_two_blocks(x_sb, 0, nc.scalar.copy)
+        second_x = turn_two_blocks(x_sb, 2, nc.vector.tensor_copy)
+        quantise_two_blocks(first_w, w_codes, w_scales, 0)
+        second_w = turn_two_blocks(w_in_sb, 2, nc.scalar.copy)
+        quantise_two_blocks(first_x, x_codes, x_scales, 0)
+        quantise_two_blocks(second_x, x_codes, x_scales, 2)
+        turn_four_blocks(w_rec_sb, w_rec_T_words, 0, nc.scalar.copy)
+        turn_four_blocks(h_sb, h_T_words, 0, nc.vector.tensor_copy)
+        turn_biases()
+        quantise_two_blocks(second_w, w_codes, w_scales, 2)
+        mx_T_of[(0, 0)] = mx_products(0, 0)
+        third_x = turn_two_blocks(x_sb, 4, nc.vector.tensor_copy)
+        fourth_x = turn_two_blocks(x_sb, 6, nc.scalar.copy)
+        quantise_two_blocks(third_x, x_codes, x_scales, 4)
+        quantise_two_blocks(fourth_x, x_codes, x_scales, 6)
+
+        waiting = []
+
+        def prepare_in_weights(gate):
+            grouped = turn_two_blocks(w_in_sb, 2 * gate, nc.vector.tensor_copy)
+            waiting.append(lambda: quantise_two_blocks(grouped, w_codes, w_scales, 2 * gate))
+
+        jobs = [lambda gate=gate: prepare_in_weights(gate) for gate in (2, 3)]
+        jobs.append(lambda: turn_four_blocks(h_sb, h_T_words, SIDE, nc.vector.tensor_copy))
+        jobs.append(lambda: turn_four_blocks(w_rec_sb, w_rec_T_words, SIDE, nc.vector.tensor_copy))
+        jobs += [lambda gate=gate: prepare_in_weights(gate) for gate in (4, 5)]
+        jobs.append(lambda: turn_four_blocks(w_rec_sb, w_rec_T_words, 2 * SIDE, nc.vector.tensor_copy))
+        jobs.append(lambda: turn_four_blocks(s_sb, s_T_words, 0, nc.vector.tensor_copy))
+        jobs.append(lambda: turn_four_blocks(s_sb, s_T_words, SIDE, nc.vector.tensor_copy))
+
+        def lagged(stage_of_step, n, lag):
+            if 0 <= n - lag < len(steps):
+                stage_of_step(*steps[n - lag])
+
+        for c in range(K_CHUNKS):
+            plain_pass(*steps[0], c)
+        for n in range(len(steps) + 4):
+            if n < len(steps):
+                pair, t = steps[n]
+                block = n // SIDE
+                if n % SIDE == MX_AT and block + 1 < N_PAIRS * N_HALVES:
+                    ahead = divmod(block + 1, N_HALVES)
+                    mx_T_of[ahead] = mx_products(*ahead)
+                for c in range(K_CHUNKS):
+                    if n + 1 < len(steps):
+                        plain_pass(*steps[n + 1], c)
+                    add_mx_product(pair, t, 2 * c)
+                    add_mx_product(pair, t, 2 * c + 1)
+                while waiting:
+                    waiting.pop(0)()
+                if n < len(jobs):
+                    jobs[n]()
+            lagged(activations, n, 1)
+            lagged(products, n, 2)
+            lagged(new_cell, n, 3)
+            lagged(new_hidden, n, 4)

@@ -24,11 +24,9 @@ N_PAIRS = N_GATES // 2
 N_RECURRENT = 4
 PAIR_COLS = 2 * HID
 GATE_TILES = N_GATES * HID // P
-PSUM_BANKS = 8
 SIDE = 4
-HALF_COLS = SIDE * P
-N_HALVES = N_TILES // SIDE
-MX_AT = 3
+AHEAD = 1
+SHARE_LAG = 4
 
 assert SIDE == 2 * K_CHUNKS
 
@@ -67,16 +65,34 @@ def tile_share_lstm_cell_kernel(
     with ExitStack() as ctx:
         keep = ctx.enter_context(tc.tile_pool(name="keep", bufs=1))
         stage = ctx.enter_context(tc.tile_pool(name="stage", bufs=3))
-        mx_pool = ctx.enter_context(tc.tile_pool(name="mx_pool", bufs=2))
-        psum = ctx.enter_context(tc.psum_pool(name="psum", bufs=PSUM_BANKS))
+        mx_pool = ctx.enter_context(tc.tile_pool(name="mx_pool", bufs=4))
+        psum_pre = ctx.enter_context(tc.psum_pool(name="psum_pre", bufs=3))
+        psum_mx = ctx.enter_context(tc.psum_pool(name="psum_mx", bufs=3))
+        psum_turn = ctx.enter_context(tc.psum_pool(name="psum_turn", bufs=2))
+        head = [True]
+
+        def turn_bank(shape, dtype):
+            if head[0]:
+                early_bank = psum_pre.tile(shape, dtype, tag="pre")
+                return early_bank
+            bank = psum_turn.tile(shape, dtype, tag="turn")
+            return bank
         ctx.enter_context(tc.manual_schedule())
 
+        zeros = keep.tile([P, PAIR_COLS], BF16)
+        nc.vector.memset(zeros[:], 0.0)
         bias_rows = keep.tile([P, P], BF16)
         nc.gpsimd.memset(bias_rows[:], 0.0)
         ident_f32 = keep.tile([P, P], F32)
         make_identity(nc, ident_f32[:])
         ident_bf16 = keep.tile([P, P], BF16)
         nc.vector.tensor_copy(out=ident_bf16[:], in_=ident_f32[:])
+
+        idle_bank = psum_mx.tile([P, PAIR_COLS], F32, tag="mx")
+
+        def keep_clock(passes):
+            for turn in range(passes):
+                nc.tensor.matmul(out=idle_bank[:], lhsT=zeros[:, 0:P], rhs=zeros[:], start=True, stop=True)
 
         x_sb = keep.tile([P, N_TILES * D_IN], BF16)
         h_sb = keep.tile([P, N_TILES * HID], BF16)
@@ -93,24 +109,18 @@ def tile_share_lstm_cell_kernel(
                 in_=by_batch_tile(dram)[:, first : first + count, :],
             )
 
-        def load_gate(tile_sb, rows, gate):
-            width = rows.shape[1]
+        def load_gates(tile_sb, weights, first, gate, count=1):
+            width = weights.shape[1]
+            rows = weights[first * HID : (first + count) * HID, :]
             nc.sync.dma_start(
-                out=tile_sb[:, gate * 2 * width : (gate + 1) * 2 * width].rearrange(
-                    "p (r n) -> p r n", r=2
+                out=tile_sb[:, gate * 2 * width : (gate + count) * 2 * width].rearrange(
+                    "p (r n) -> p r n", n=width
                 ),
                 in_=rows.rearrange("(r p) n -> p r n", p=P),
             )
 
-        def load_in_weights(gate):
-            load_gate(w_in_sb, weight_ih[gate * HID : (gate + 1) * HID, :], gate)
-
-        def load_recurrent_weights(gate):
-            if gate < N_RECURRENT:
-                load_gate(w_rec_sb, weight_hh[gate * HID : (gate + 1) * HID, :], gate)
-            else:
-                share = gate - N_RECURRENT
-                load_gate(w_rec_sb, weight_sh[share * HID : (share + 1) * HID, :], gate)
+        def load_in_weights(gate, count=1):
+            load_gates(w_in_sb, weight_ih, gate, gate, count)
 
         def as_rows(vector):
             return vector.rearrange("(r n) -> r n", n=P)
@@ -121,32 +131,28 @@ def tile_share_lstm_cell_kernel(
         nc.scalar.activation(out=warm[:], in_=warm[:], func=ACT.Sigmoid)
         load_in_weights(0)
         load_batch(x_sb, x, 0, 2)
-        load_batch(x_sb, x, 2, 2)
         load_in_weights(1)
+        load_gates(w_rec_sb, weight_hh, 0, 0, 2)
+        load_batch(h_sb, h_minors, 0, SIDE)
         nc.sync.dma_start(out=bias_rows[0:GATE_TILES, :], in_=as_rows(bias_ih))
         nc.sync.dma_start(out=bias_rows[GATE_TILES : GATE_TILES + rec_rows, :], in_=as_rows(bias_hh))
         nc.sync.dma_start(out=bias_rows[GATE_TILES + rec_rows : 2 * GATE_TILES, :], in_=as_rows(bias_sh))
-        load_recurrent_weights(0)
-        load_recurrent_weights(1)
-        load_batch(h_sb, h_minors, 0, SIDE)
+        load_batch(x_sb, x, 2, 2)
         load_batch(x_sb, x, SIDE, SIDE)
-        load_in_weights(2)
-        load_in_weights(3)
         load_batch(h_sb, h_minors, SIDE, SIDE)
-        load_recurrent_weights(2)
-        load_recurrent_weights(3)
+        load_in_weights(2)
         nc.sync.dma_start(out=mask_sb[:], in_=mask.rearrange("(p t) -> p t", t=N_TILES))
         nc.sync.dma_start(out=c_sb[:], in_=by_batch_tile(c_minors))
-        load_in_weights(4)
-        load_in_weights(5)
-        load_recurrent_weights(4)
-        load_recurrent_weights(5)
+        load_in_weights(3)
+        load_gates(w_rec_sb, weight_hh, 2, 2, 2)
+        load_in_weights(4, 2)
+        load_gates(w_rec_sb, weight_sh, 0, N_RECURRENT, 2)
         load_batch(s_sb, s_minors[idx, :, :], 0, N_TILES)
 
         bias_col = keep.tile([P, GATE_TILES], F32)
 
         def turn_biases():
-            bias_turned = psum.tile([P, P], BF16, tag="bank")
+            bias_turned = turn_bank([P, P], BF16)
             nc.tensor.transpose(bias_turned[:], bias_rows[:], ident_bf16[:])
             bias_parts = keep.tile([P, 2 * GATE_TILES], F32)
             nc.vector.tensor_copy(out=bias_parts[:], in_=bias_turned[:, 0 : 2 * GATE_TILES])
@@ -168,14 +174,17 @@ def tile_share_lstm_cell_kernel(
         s_T = s_T_words[:].bitcast(BF16).rearrange("p (t b e) -> p t b e", t=N_TILES, e=2)
         w_rec_T = w_rec_T_words[:].bitcast(BF16).rearrange("p (g n e) -> p g n e", g=N_PAIRS, e=2)
 
-        def turn_two_blocks(source_sb, first_block, copy_out):
+        def turn_two_blocks(source_sb, first_block):
             words = source_sb[:].bitcast(F32)
-            turned = psum.tile([P, 2, 2, P], F32, tag="bank")
+            turned = turn_bank([P, 2, 2, P], F32)
             for j in range(2):
                 for u in range(2):
                     first = (first_block + j) * WORDS + u
                     last = (first_block + j + 1) * WORDS
                     nc.tensor.transpose(turned[:, j, u, :], words[:, first:last:2], ident_f32[:])
+            return turned
+
+        def group_two_blocks(turned, copy_out):
             grouped = stage.tile([P, 2 * P * PACK], BF16, align_bytes=64)
             copy_out(
                 out=grouped[:].bitcast(F32).rearrange("p (j r u) -> p j r u", j=2, u=2),
@@ -189,24 +198,30 @@ def tile_share_lstm_cell_kernel(
                 out=codes[:, cols].bitcast(FP8X4), scales=scales[:, cols], in_=grouped[:]
             )
 
-        def turn_four_blocks(source_sb, dest_words, first_block, copy_out):
+        def turn_four_blocks(source_sb, first_block):
             words = source_sb[:].bitcast(F32)
-            turned = psum.tile([P, SIDE * P], F32, tag="bank")
+            turned = turn_bank([P, SIDE * P], F32)
             for i in range(SIDE):
                 cols = slice((first_block + i) * P, (first_block + i + 1) * P)
                 nc.tensor.transpose(turned[:, i * P : (i + 1) * P], words[:, cols], ident_f32[:])
+            return turned
+
+        def copy_four_blocks(turned, dest_words, first_block, copy_out):
             copy_out(out=dest_words[:, first_block * P : (first_block + SIDE) * P], in_=turned[:])
 
-        def mx_products(pair, half):
-            mx_T = mx_pool.tile([P, SIDE, HALF_COLS], F32)
-            batch = slice(half * HALF_COLS, (half + 1) * HALF_COLS)
-            banks = []
-            for j in range(SIDE):
-                gate_tile = SIDE * pair + j
-                rows = slice(gate_tile * P, (gate_tile + 1) * P)
-                acc_mx = psum.tile([P, HALF_COLS], F32, tag="bank")
+        mx_T_of = {}
+
+        def tiles_of_block(pair):
+            return 2 if pair == 0 else SIDE
+
+        def mx_bank(pair, first, gate_tiles):
+            width = tiles_of_block(pair) * P
+            batch = slice(first * P, first * P + width)
+            bank = psum_mx.tile([P, PAIR_COLS], F32, tag="mx")
+            for i, j in enumerate(gate_tiles):
+                rows = slice((SIDE * pair + j) * P, (SIDE * pair + j + 1) * P)
                 nc.tensor.matmul_mx(
-                    out=acc_mx[:],
+                    out=bank[:, i * width : (i + 1) * width],
                     lhsT=w_codes[:, rows].bitcast(FP8X4),
                     lhsT_scale=w_scales[:, rows],
                     rhs=x_codes[:, batch].bitcast(FP8X4),
@@ -214,28 +229,34 @@ def tile_share_lstm_cell_kernel(
                     start=True,
                     stop=True,
                 )
-                banks.append(acc_mx)
-            for j in range(SIDE):
-                bias = bias_col[:, SIDE * pair + j : SIDE * pair + j + 1]
-                if j % 2 == 0:
-                    nc.scalar.activation(out=mx_T[:, j, :], in_=banks[j][:], func=ACT.Identity, bias=bias)
-                else:
-                    nc.vector.tensor_scalar_add(out=mx_T[:, j, :], in0=banks[j][:], scalar1=bias)
-            return mx_T
+            return bank
 
-        steps = [
-            (pair, half * SIDE + q)
-            for pair in range(N_PAIRS)
-            for half in range(N_HALVES)
-            for q in range(SIDE)
-        ]
-        gates = keep.tile([P, N_PAIRS, N_TILES, PAIR_COLS], F32)
-        mx_T_of = {}
+        def mx_out(pair, first, gate_tiles, bank, on_scalar):
+            width = tiles_of_block(pair) * P
+            if gate_tiles[0] == 0:
+                mx_T_block = mx_pool.tile([P, SIDE, SIDE * P], F32)
+                mx_T_of[(pair, first)] = mx_T_block
+            mx_T = mx_T_of[(pair, first)]
+            for i, j in enumerate(gate_tiles):
+                bias = bias_col[:, SIDE * pair + j : SIDE * pair + j + 1]
+                product = bank[:, i * width : (i + 1) * width]
+                if on_scalar:
+                    nc.scalar.activation(out=mx_T[:, j, 0:width], in_=product, func=ACT.Identity, bias=bias)
+                else:
+                    nc.vector.tensor_scalar_add(out=mx_T[:, j, 0:width], in0=product, scalar1=bias)
+
+        steps = [(0, t) for t in range(N_TILES)]
+        for t in range(N_TILES + SHARE_LAG):
+            if t < N_TILES:
+                steps.append((1, t))
+            if t >= SHARE_LAG:
+                steps.append((2, t - SHARE_LAG))
         pre_of = {}
+        gates = keep.tile([P, N_PAIRS, N_TILES, PAIR_COLS], F32)
 
         def plain_pass(pair, t, c):
             if c == 0:
-                bank = psum.tile([P, PAIR_COLS], F32, tag="bank")
+                bank = psum_pre.tile([P, PAIR_COLS], F32, tag="pre")
                 pre_of[(pair, t)] = bank
             state_T = h_T if 2 * pair < N_RECURRENT else s_T
             nc.tensor.matmul(
@@ -247,10 +268,11 @@ def tile_share_lstm_cell_kernel(
             )
 
         def add_mx_product(pair, t, j):
-            q = t % SIDE
+            tiles = tiles_of_block(pair)
+            q = t % tiles
             nc.tensor.matmul(
                 out=pre_of[(pair, t)][:, j * P : (j + 1) * P],
-                lhsT=mx_T_of[(pair, t // SIDE)][:, j, q * P : (q + 1) * P],
+                lhsT=mx_T_of[(pair, t - q)][:, j, q * P : (q + 1) * P],
                 rhs=ident_f32[:],
                 is_transpose=True,
                 start=False,
@@ -265,8 +287,8 @@ def tile_share_lstm_cell_kernel(
             else:
                 nc.scalar.activation(out=gates[:, pair, t, :], in_=pre[:], func=ACT.Sigmoid)
 
+        masked_c = keep.tile([P, N_TILES, HID], F32)
         kept = keep.tile([P, N_TILES, HID], F32)
-        cell = keep.tile([P, N_TILES, HID], F32)
         squashed = keep.tile([P, N_TILES, HID], F32)
         h_res = keep.tile([P, N_TILES, HID], F32)
         c_res = keep.tile([P, N_TILES, HID], F32)
@@ -275,99 +297,162 @@ def tile_share_lstm_cell_kernel(
         def store(dram, result, t):
             nc.sync.dma_start(out=by_batch_tile(dram)[:, t, :], in_=result[:, t, :])
 
-        def times_masked_tanh(out, gate, t):
+        def masked_product(out, in0, in1, t):
             nc.vector.scalar_tensor_tensor(
-                out=out,
-                in0=squashed[:, t, :],
-                scalar=mask_f32[:, t : t + 1],
-                in1=gate,
-                op0=ALU.mult,
-                op1=ALU.mult,
+                out=out, in0=in0, scalar=mask_f32[:, t : t + 1], in1=in1, op0=ALU.mult, op1=ALU.mult
             )
+
+        in_term_of = {}
 
         def products(pair, t):
             if pair == 0:
-                nc.vector.tensor_tensor(
-                    out=kept[:, t, :], in0=gates[:, 0, t, HID:], in1=c_sb[:, t, :], op=ALU.mult
+                nc.gpsimd.tensor_scalar(
+                    out=masked_c[:, t, :],
+                    in0=c_sb[:, t, :],
+                    scalar1=mask_f32[:, t : t + 1],
+                    scalar2=0.0,
+                    op0=ALU.mult,
+                    op1=ALU.add,
+                )
+                nc.gpsimd.tensor_tensor(
+                    out=kept[:, t, :], in0=gates[:, 0, t, HID:], in1=masked_c[:, t, :], op=ALU.mult
                 )
             elif pair == 1:
                 in_term = stage.tile([P, HID], F32)
-                nc.vector.tensor_tensor(
+                in_term_of[t] = in_term
+                nc.gpsimd.tensor_tensor(
                     out=in_term[:], in0=gates[:, 0, t, 0:HID], in1=gates[:, 1, t, HID:], op=ALU.mult
                 )
-                nc.vector.tensor_tensor(out=cell[:, t, :], in0=in_term[:], in1=kept[:, t, :], op=ALU.add)
             else:
-                for share in range(2):
-                    times_masked_tanh(s_res[:, share, t, :], gates[:, 2, t, share * HID : (share + 1) * HID], t)
+                masked_product(
+                    s_res[:, :, t, :],
+                    squashed[:, t, :].unsqueeze(1).to_broadcast([P, 2, HID]),
+                    gates[:, 2, t, :].rearrange("p (s n) -> p s n", s=2),
+                    t,
+                )
                 store(out_s0, s_res[:, 0, :, :], t)
                 store(out_s1, s_res[:, 1, :, :], t)
 
         def new_cell(pair, t):
             if pair == 1:
-                m = mask_f32[:, t : t + 1]
-                nc.scalar.activation(out=squashed[:, t, :], in_=cell[:, t, :], func=ACT.Tanh, scale=m)
-                nc.vector.tensor_scalar_mul(out=c_res[:, t, :], in0=cell[:, t, :], scalar1=m)
+                nc.vector.scalar_tensor_tensor(
+                    out=c_res[:, t, :],
+                    in0=in_term_of[t][:],
+                    scalar=mask_f32[:, t : t + 1],
+                    in1=kept[:, t, :],
+                    op0=ALU.mult,
+                    op1=ALU.add,
+                )
                 store(out_c, c_res, t)
+
+        def squash(pair, t):
+            if pair == 1:
+                nc.scalar.activation(out=squashed[:, t, :], in_=c_res[:, t, :], func=ACT.Tanh)
 
         def new_hidden(pair, t):
             if pair == 1:
-                times_masked_tanh(h_res[:, t, :], gates[:, 1, t, 0:HID], t)
+                masked_product(h_res[:, t, :], squashed[:, t, :], gates[:, 1, t, 0:HID], t)
                 store(out_h, h_res, t)
 
-        first_w = turn_two_blocks(w_in_sb, 0, nc.vector.tensor_copy)
-        first_x = turn_two_blocks(x_sb, 0, nc.scalar.copy)
-        second_x = turn_two_blocks(x_sb, 2, nc.vector.tensor_copy)
+        keep_clock(3)
+        w_turned = turn_two_blocks(w_in_sb, 0)
+        keep_clock(1)
+        first_w = group_two_blocks(w_turned, nc.vector.tensor_copy)
+        x_turned = turn_two_blocks(x_sb, 0)
+        keep_clock(1)
+        first_x = group_two_blocks(x_turned, nc.scalar.copy)
         quantise_two_blocks(first_w, w_codes, w_scales, 0)
-        second_w = turn_two_blocks(w_in_sb, 2, nc.scalar.copy)
+        w_turned = turn_two_blocks(w_in_sb, 2)
+        keep_clock(1)
+        second_w = group_two_blocks(w_turned, nc.vector.tensor_copy)
         quantise_two_blocks(first_x, x_codes, x_scales, 0)
-        quantise_two_blocks(second_x, x_codes, x_scales, 2)
-        turn_four_blocks(w_rec_sb, w_rec_T_words, 0, nc.scalar.copy)
-        turn_four_blocks(h_sb, h_T_words, 0, nc.vector.tensor_copy)
-        turn_biases()
+        rec_turned = turn_four_blocks(w_rec_sb, 0)
+        keep_clock(1)
+        copy_four_blocks(rec_turned, w_rec_T_words, 0, nc.scalar.copy)
+        h_turned = turn_four_blocks(h_sb, 0)
+        keep_clock(1)
+        copy_four_blocks(h_turned, h_T_words, 0, nc.scalar.copy)
         quantise_two_blocks(second_w, w_codes, w_scales, 2)
-        mx_T_of[(0, 0)] = mx_products(0, 0)
-        third_x = turn_two_blocks(x_sb, 4, nc.vector.tensor_copy)
-        fourth_x = turn_two_blocks(x_sb, 6, nc.scalar.copy)
-        quantise_two_blocks(third_x, x_codes, x_scales, 4)
-        quantise_two_blocks(fourth_x, x_codes, x_scales, 6)
+        x_turned = turn_two_blocks(x_sb, 2)
+        turn_biases()
+        second_x = group_two_blocks(x_turned, nc.vector.tensor_copy)
 
-        waiting = []
+        mx_at = {}
+        for n, (pair, t) in enumerate(steps):
+            if t % tiles_of_block(pair) == 0:
+                fills = [(0, 1), (2, 3)] if pair == 0 else [(j,) for j in range(SIDE)]
+                for i, gate_tiles in enumerate(fills):
+                    mx_at.setdefault(n - 1 - len(fills) + i, []).append((pair, t, gate_tiles))
 
-        def prepare_in_weights(gate):
-            grouped = turn_two_blocks(w_in_sb, 2 * gate, nc.vector.tensor_copy)
-            waiting.append(lambda: quantise_two_blocks(grouped, w_codes, w_scales, 2 * gate))
+        def quantised(source_sb, first, codes, scales, copy_out):
+            made = []
+            return [
+                lambda: made.append(turn_two_blocks(source_sb, first)),
+                lambda: made.append(group_two_blocks(made[0], copy_out)),
+                lambda: quantise_two_blocks(made[1], codes, scales, first),
+            ]
 
-        jobs = [lambda gate=gate: prepare_in_weights(gate) for gate in (2, 3)]
-        jobs.append(lambda: turn_four_blocks(h_sb, h_T_words, SIDE, nc.vector.tensor_copy))
-        jobs.append(lambda: turn_four_blocks(w_rec_sb, w_rec_T_words, SIDE, nc.vector.tensor_copy))
-        jobs += [lambda gate=gate: prepare_in_weights(gate) for gate in (4, 5)]
-        jobs.append(lambda: turn_four_blocks(w_rec_sb, w_rec_T_words, 2 * SIDE, nc.vector.tensor_copy))
-        jobs.append(lambda: turn_four_blocks(s_sb, s_T_words, 0, nc.vector.tensor_copy))
-        jobs.append(lambda: turn_four_blocks(s_sb, s_T_words, SIDE, nc.vector.tensor_copy))
+        def turned_words(source_sb, first, dest_words, copy_out):
+            made = []
+            return [
+                lambda: made.append(turn_four_blocks(source_sb, first)),
+                lambda: copy_four_blocks(made[0], dest_words, first, copy_out),
+            ]
+
+        on_vector = nc.vector.tensor_copy
+        on_scalar = nc.scalar.copy
+        jobs = [
+            (-2, quantised(x_sb, 4, x_codes, x_scales, on_vector)),
+            (-1, quantised(w_in_sb, 4, w_codes, w_scales, on_vector)),
+            (0, quantised(x_sb, 6, x_codes, x_scales, on_scalar)),
+            (1, turned_words(h_sb, SIDE, h_T_words, on_scalar)),
+            (2, quantised(w_in_sb, 6, w_codes, w_scales, on_vector)),
+            (4, turned_words(w_rec_sb, SIDE, w_rec_T_words, on_scalar)),
+            (5, quantised(w_in_sb, 8, w_codes, w_scales, on_vector)),
+            (7, quantised(w_in_sb, 10, w_codes, w_scales, on_vector)),
+            (9, turned_words(w_rec_sb, 2 * SIDE, w_rec_T_words, on_vector)),
+            (10, turned_words(s_sb, 0, s_T_words, on_vector)),
+            (14, turned_words(s_sb, SIDE, s_T_words, on_vector)),
+        ]
+        parts_at = {}
+        parts_at[-2] = [(2, lambda: quantise_two_blocks(second_x, x_codes, x_scales, 2))]
+        for start, parts in jobs:
+            for i, part in enumerate(parts):
+                parts_at.setdefault(start + i, []).append((i, part))
+
+        def do_parts(n, number):
+            for i, part in parts_at.get(n, []):
+                if i == number:
+                    part()
 
         def lagged(stage_of_step, n, lag):
             if 0 <= n - lag < len(steps):
                 stage_of_step(*steps[n - lag])
 
-        for c in range(K_CHUNKS):
-            plain_pass(*steps[0], c)
-        for n in range(len(steps) + 4):
-            if n < len(steps):
-                pair, t = steps[n]
-                block = n // SIDE
-                if n % SIDE == MX_AT and block + 1 < N_PAIRS * N_HALVES:
-                    ahead = divmod(block + 1, N_HALVES)
-                    mx_T_of[ahead] = mx_products(*ahead)
-                for c in range(K_CHUNKS):
-                    if n + 1 < len(steps):
-                        plain_pass(*steps[n + 1], c)
-                    add_mx_product(pair, t, 2 * c)
-                    add_mx_product(pair, t, 2 * c + 1)
-                while waiting:
-                    waiting.pop(0)()
-                if n < len(jobs):
-                    jobs[n]()
+        head[0] = False
+        full_banks = []
+        turns = 0
+        for n in range(-3, len(steps) + 5):
+            coming = n + AHEAD
+            filled = []
+            if 0 <= coming < len(steps):
+                plain_pass(*steps[coming], 0)
+            for fill in mx_at.get(n, []):
+                filled.append((*fill, mx_bank(*fill)))
+            if 0 <= coming < len(steps):
+                plain_pass(*steps[coming], 1)
+            if 0 <= n < len(steps):
+                for j in range(SIDE):
+                    add_mx_product(*steps[n], j)
             lagged(activations, n, 1)
+            for full in full_banks:
+                mx_out(*full, turns % 2 == 0)
+                turns += 1
+            full_banks = filled
             lagged(products, n, 2)
             lagged(new_cell, n, 3)
-            lagged(new_hidden, n, 4)
+            do_parts(n, 1)
+            do_parts(n, 2)
+            do_parts(n, 0)
+            lagged(squash, n, 4)
+            lagged(new_hidden, n, 5)

@@ -90,9 +90,11 @@ def tile_share_lstm_cell_kernel(
 
         idle_bank = psum_mx.tile([P, PAIR_COLS], F32, tag="mx")
 
-        def keep_clock(passes):
+        def keep_clock(passes, width=PAIR_COLS):
             for turn in range(passes):
-                nc.tensor.matmul(out=idle_bank[:], lhsT=zeros[:, 0:P], rhs=zeros[:], start=True, stop=True)
+                nc.tensor.matmul(
+                    out=idle_bank[:, 0:width], lhsT=zeros[:, 0:P], rhs=zeros[:, 0:width], start=True, stop=True
+                )
 
         x_sb = keep.tile([P, N_TILES * D_IN], BF16)
         h_sb = keep.tile([P, N_TILES * HID], BF16)
@@ -279,11 +281,18 @@ def tile_share_lstm_cell_kernel(
                 stop=(j == SIDE - 1),
             )
 
+        def is_last(pair, t):
+            return (pair, t) == steps[-1]
+
         def activations(pair, t):
             pre = pre_of[(pair, t)]
             if pair == 1:
                 nc.scalar.activation(out=gates[:, pair, t, 0:HID], in_=pre[:, 0:HID], func=ACT.Sigmoid)
                 nc.scalar.activation(out=gates[:, pair, t, HID:], in_=pre[:, HID:], func=ACT.Tanh)
+            elif is_last(pair, t):
+                for share in range(2):
+                    cols = slice(share * HID, (share + 1) * HID)
+                    nc.scalar.activation(out=gates[:, pair, t, cols], in_=pre[:, cols], func=ACT.Sigmoid)
             else:
                 nc.scalar.activation(out=gates[:, pair, t, :], in_=pre[:], func=ACT.Sigmoid)
 
@@ -324,14 +333,16 @@ def tile_share_lstm_cell_kernel(
                     out=in_term[:], in0=gates[:, 0, t, 0:HID], in1=gates[:, 1, t, HID:], op=ALU.mult
                 )
             else:
-                masked_product(
-                    s_res[:, :, t, :],
-                    squashed[:, t, :].unsqueeze(1).to_broadcast([P, 2, HID]),
-                    gates[:, 2, t, :].rearrange("p (s n) -> p s n", s=2),
-                    t,
-                )
-                store(out_s0, s_res[:, 0, :, :], t)
-                store(out_s1, s_res[:, 1, :, :], t)
+                for shares in [slice(0, 1), slice(1, 2)] if is_last(pair, t) else [slice(0, 2)]:
+                    count = shares.stop - shares.start
+                    masked_product(
+                        s_res[:, shares, t, :],
+                        squashed[:, t, :].unsqueeze(1).to_broadcast([P, count, HID]),
+                        gates[:, 2, t, :].rearrange("p (s n) -> p s n", s=2)[:, shares, :],
+                        t,
+                    )
+                    for share in range(shares.start, shares.stop):
+                        store((out_s0, out_s1)[share], s_res[:, share, :, :], t)
 
         def new_cell(pair, t):
             if pair == 1:
@@ -356,25 +367,24 @@ def tile_share_lstm_cell_kernel(
 
         keep_clock(3)
         w_turned = turn_two_blocks(w_in_sb, 0)
-        keep_clock(1)
+        keep_clock(1, HID)
         first_w = group_two_blocks(w_turned, nc.vector.tensor_copy)
         x_turned = turn_two_blocks(x_sb, 0)
-        keep_clock(1)
+        keep_clock(1, HID)
         first_x = group_two_blocks(x_turned, nc.scalar.copy)
         quantise_two_blocks(first_w, w_codes, w_scales, 0)
         w_turned = turn_two_blocks(w_in_sb, 2)
-        keep_clock(1)
-        second_w = group_two_blocks(w_turned, nc.vector.tensor_copy)
+        keep_clock(1, HID)
+        second_w = group_two_blocks(w_turned, nc.scalar.copy)
         quantise_two_blocks(first_x, x_codes, x_scales, 0)
         rec_turned = turn_four_blocks(w_rec_sb, 0)
-        keep_clock(1)
-        copy_four_blocks(rec_turned, w_rec_T_words, 0, nc.scalar.copy)
+        keep_clock(1, HID)
         h_turned = turn_four_blocks(h_sb, 0)
-        keep_clock(1)
-        copy_four_blocks(h_turned, h_T_words, 0, nc.scalar.copy)
+        keep_clock(1, HID)
         quantise_two_blocks(second_w, w_codes, w_scales, 2)
+        copy_four_blocks(rec_turned, w_rec_T_words, 0, nc.vector.tensor_copy)
+        copy_four_blocks(h_turned, h_T_words, 0, nc.scalar.copy)
         x_turned = turn_two_blocks(x_sb, 2)
-        turn_biases()
         second_x = group_two_blocks(x_turned, nc.vector.tensor_copy)
 
         mx_at = {}
@@ -405,14 +415,14 @@ def tile_share_lstm_cell_kernel(
             (-2, quantised(x_sb, 4, x_codes, x_scales, on_vector)),
             (-1, quantised(w_in_sb, 4, w_codes, w_scales, on_vector)),
             (0, quantised(x_sb, 6, x_codes, x_scales, on_scalar)),
-            (1, turned_words(h_sb, SIDE, h_T_words, on_scalar)),
+            (1, turned_words(h_sb, SIDE, h_T_words, on_vector)),
             (2, quantised(w_in_sb, 6, w_codes, w_scales, on_vector)),
             (4, turned_words(w_rec_sb, SIDE, w_rec_T_words, on_scalar)),
             (5, quantised(w_in_sb, 8, w_codes, w_scales, on_vector)),
             (7, quantised(w_in_sb, 10, w_codes, w_scales, on_vector)),
             (9, turned_words(w_rec_sb, 2 * SIDE, w_rec_T_words, on_vector)),
             (10, turned_words(s_sb, 0, s_T_words, on_vector)),
-            (14, turned_words(s_sb, SIDE, s_T_words, on_vector)),
+            (14, turned_words(s_sb, SIDE, s_T_words, on_scalar)),
         ]
         parts_at = {}
         parts_at[-2] = [(2, lambda: quantise_two_blocks(second_x, x_codes, x_scales, 2))]
@@ -439,14 +449,16 @@ def tile_share_lstm_cell_kernel(
                 plain_pass(*steps[coming], 0)
             for fill in mx_at.get(n, []):
                 filled.append((*fill, mx_bank(*fill)))
+            if n == -3:
+                turn_biases()
             if 0 <= coming < len(steps):
                 plain_pass(*steps[coming], 1)
             if 0 <= n < len(steps):
                 for j in range(SIDE):
                     add_mx_product(*steps[n], j)
             lagged(activations, n, 1)
-            for full in full_banks:
-                mx_out(*full, turns % 2 == 0)
+            for i, full in enumerate(full_banks):
+                mx_out(*full, turns % 2 == 0 if n < N_TILES else i == 1)
                 turns += 1
             full_banks = filled
             lagged(products, n, 2)

@@ -90,11 +90,9 @@ def tile_share_lstm_cell_kernel(
 
         idle_bank = psum_mx.tile([P, PAIR_COLS], F32, tag="mx")
 
-        def keep_clock(passes, width=PAIR_COLS):
+        def keep_clock(passes):
             for turn in range(passes):
-                nc.tensor.matmul(
-                    out=idle_bank[:, 0:width], lhsT=zeros[:, 0:P], rhs=zeros[:, 0:width], start=True, stop=True
-                )
+                nc.tensor.matmul(out=idle_bank[:], lhsT=zeros[:, 0:P], rhs=zeros[:], start=True, stop=True)
 
         x_sb = keep.tile([P, N_TILES * D_IN], BF16)
         h_sb = keep.tile([P, N_TILES * HID], BF16)
@@ -329,9 +327,7 @@ def tile_share_lstm_cell_kernel(
             elif pair == 1:
                 in_term = stage.tile([P, HID], F32)
                 in_term_of[t] = in_term
-                nc.gpsimd.tensor_tensor(
-                    out=in_term[:], in0=gates[:, 0, t, 0:HID], in1=gates[:, 1, t, HID:], op=ALU.mult
-                )
+                masked_product(in_term[:], gates[:, 0, t, 0:HID], gates[:, 1, t, HID:], t)
             else:
                 for shares in [slice(0, 1), slice(1, 2)] if is_last(pair, t) else [slice(0, 2)]:
                     count = shares.stop - shares.start
@@ -346,13 +342,8 @@ def tile_share_lstm_cell_kernel(
 
         def new_cell(pair, t):
             if pair == 1:
-                nc.vector.scalar_tensor_tensor(
-                    out=c_res[:, t, :],
-                    in0=in_term_of[t][:],
-                    scalar=mask_f32[:, t : t + 1],
-                    in1=kept[:, t, :],
-                    op0=ALU.mult,
-                    op1=ALU.add,
+                nc.vector.tensor_tensor(
+                    out=c_res[:, t, :], in0=in_term_of[t][:], in1=kept[:, t, :], op=ALU.add
                 )
                 store(out_c, c_res, t)
 
@@ -367,20 +358,20 @@ def tile_share_lstm_cell_kernel(
 
         keep_clock(3)
         w_turned = turn_two_blocks(w_in_sb, 0)
-        keep_clock(1, HID)
+        keep_clock(1)
         first_w = group_two_blocks(w_turned, nc.vector.tensor_copy)
         x_turned = turn_two_blocks(x_sb, 0)
-        keep_clock(1, HID)
+        keep_clock(1)
         first_x = group_two_blocks(x_turned, nc.scalar.copy)
         quantise_two_blocks(first_w, w_codes, w_scales, 0)
         w_turned = turn_two_blocks(w_in_sb, 2)
-        keep_clock(1, HID)
+        keep_clock(1)
         second_w = group_two_blocks(w_turned, nc.scalar.copy)
         quantise_two_blocks(first_x, x_codes, x_scales, 0)
         rec_turned = turn_four_blocks(w_rec_sb, 0)
-        keep_clock(1, HID)
+        keep_clock(1)
         h_turned = turn_four_blocks(h_sb, 0)
-        keep_clock(1, HID)
+        keep_clock(1)
         quantise_two_blocks(second_w, w_codes, w_scales, 2)
         copy_four_blocks(rec_turned, w_rec_T_words, 0, nc.vector.tensor_copy)
         copy_four_blocks(h_turned, h_T_words, 0, nc.scalar.copy)
@@ -457,8 +448,8 @@ def tile_share_lstm_cell_kernel(
                 for j in range(SIDE):
                     add_mx_product(*steps[n], j)
             lagged(activations, n, 1)
-            for i, full in enumerate(full_banks):
-                mx_out(*full, turns % 2 == 0 if n < N_TILES else i == 1)
+            for full in full_banks:
+                mx_out(*full, turns % 2 == 0)
                 turns += 1
             full_banks = filled
             lagged(products, n, 2)

@@ -174,6 +174,22 @@ def tile_share_lstm_cell_kernel(
         s_T = s_T_words[:].bitcast(BF16).rearrange("p (t b e) -> p t b e", t=N_TILES, e=2)
         w_rec_T = w_rec_T_words[:].bitcast(BF16).rearrange("p (g n e) -> p g n e", g=N_PAIRS, e=2)
 
+        def parted_words(source_sb, first_block):
+            parted = stage.tile([P, 2, 2, P], F32)
+            cols = slice(first_block * WORDS, (first_block + 2) * WORDS)
+            nc.vector.tensor_copy(
+                out=parted[:],
+                in_=source_sb[:].bitcast(F32)[:, cols].rearrange("p (j w u) -> p j u w", j=2, u=2),
+            )
+            return parted
+
+        def turn_parted(parted):
+            turned = turn_bank([P, 2, 2, P], F32)
+            for j in range(2):
+                for u in range(2):
+                    nc.tensor.transpose(turned[:, j, u, :], parted[:, j, u, :], ident_f32[:])
+            return turned
+
         def turn_two_blocks(source_sb, first_block):
             words = source_sb[:].bitcast(F32)
             turned = turn_bank([P, 2, 2, P], F32)
@@ -393,6 +409,15 @@ def tile_share_lstm_cell_kernel(
                 lambda: quantise_two_blocks(made[1], codes, scales, first),
             ]
 
+        def parted_and_quantised(source_sb, first, codes, scales, copy_out):
+            made = []
+            return [
+                lambda: made.append(parted_words(source_sb, first)),
+                lambda: made.append(turn_parted(made[0])),
+                lambda: made.append(group_two_blocks(made[1], copy_out)),
+                lambda: quantise_two_blocks(made[2], codes, scales, first),
+            ]
+
         def turned_words(source_sb, first, dest_words, copy_out):
             made = []
             return [
@@ -407,10 +432,10 @@ def tile_share_lstm_cell_kernel(
             (-1, quantised(w_in_sb, 4, w_codes, w_scales, on_vector)),
             (0, quantised(x_sb, 6, x_codes, x_scales, on_scalar)),
             (1, turned_words(h_sb, SIDE, h_T_words, on_vector)),
-            (2, quantised(w_in_sb, 6, w_codes, w_scales, on_vector)),
+            (2, parted_and_quantised(w_in_sb, 6, w_codes, w_scales, on_vector)),
             (4, turned_words(w_rec_sb, SIDE, w_rec_T_words, on_scalar)),
-            (5, quantised(w_in_sb, 8, w_codes, w_scales, on_vector)),
-            (7, quantised(w_in_sb, 10, w_codes, w_scales, on_vector)),
+            (5, parted_and_quantised(w_in_sb, 8, w_codes, w_scales, on_vector)),
+            (7, parted_and_quantised(w_in_sb, 10, w_codes, w_scales, on_vector)),
             (9, turned_words(w_rec_sb, 2 * SIDE, w_rec_T_words, on_vector)),
             (10, turned_words(s_sb, 0, s_T_words, on_vector)),
             (14, turned_words(s_sb, SIDE, s_T_words, on_scalar)),
@@ -418,7 +443,7 @@ def tile_share_lstm_cell_kernel(
         parts_at = {}
         parts_at[-2] = [(2, lambda: quantise_two_blocks(second_x, x_codes, x_scales, 2))]
         for start, parts in jobs:
-            for i, part in enumerate(parts):
+            for i, part in enumerate(parts, -1 if len(parts) == 4 else 0):
                 parts_at.setdefault(start + i, []).append((i, part))
 
         def do_parts(n, number):
@@ -457,5 +482,6 @@ def tile_share_lstm_cell_kernel(
             do_parts(n, 1)
             do_parts(n, 2)
             do_parts(n, 0)
+            do_parts(n, -1)
             lagged(squash, n, 4)
             lagged(new_hidden, n, 5)

from contextlib import ExitStack

import concourse.mybir as mybir
from concourse.masks import make_identity

FP8X4 = mybir.dt.float8_e4m3fn_x4
BF16 = mybir.dt.bfloat16
F32 = mybir.dt.float32
U32 = mybir.dt.uint32
U8 = mybir.dt.uint8
ACT = mybir.ActivationFunctionType
ALU = mybir.AluOpType

P = 128
PACK = 4
BATCH = 1024
D_IN = 512
HID = 256
N_TILES = BATCH // P
WORDS = D_IN // 2
K_CHUNKS = HID // P
N_GATES = 6
N_PAIRS = N_GATES // 2
N_RECURRENT = 4
PAIR_COLS = 2 * HID
GATE_TILES = N_GATES * HID // P
SIDE = 4
AHEAD = 1
SHARE_LAG = 4

assert SIDE == 2 * K_CHUNKS

FLOPS = 2 * BATCH * (D_IN * N_GATES * HID + HID * N_GATES * HID)
BYTES = (
    2 * (BATCH * D_IN + 3 * BATCH * HID + BATCH)
    + 2 * (N_GATES * HID * (D_IN + HID) + 2 * N_GATES * HID)
    + 4 * 4 * BATCH * HID
)


def tile_share_lstm_cell_kernel(
    tc,
    x,
    h_minors,
    c_minors,
    s_minors,
    mask,
    weight_ih,
    weight_hh,
    weight_sh,
    bias_ih,
    bias_hh,
    bias_sh,
    idx,
    out_h,
    out_c,
    out_s0,
    out_s1,
):
    nc = tc.nc

    def by_batch_tile(dram):
        return dram.rearrange("(p t) n -> p t n", t=N_TILES)

    with ExitStack() as ctx:
        keep = ctx.enter_context(tc.tile_pool(name="keep", bufs=1))
        stage = ctx.enter_context(tc.tile_pool(name="stage", bufs=3))
        mx_pool = ctx.enter_context(tc.tile_pool(name="mx_pool", bufs=4))
        psum_pre = ctx.enter_context(tc.psum_pool(name="psum_pre", bufs=3))
        psum_mx = ctx.enter_context(tc.psum_pool(name="psum_mx", bufs=3))
        psum_turn = ctx.enter_context(tc.psum_pool(name="psum_turn", bufs=2))
        head = [True]

        def turn_bank(shape, dtype):
            if head[0]:
                early_bank = psum_pre.tile(shape, dtype, tag="pre")
                return early_bank
            bank = psum_turn.tile(shape, dtype, tag="turn")
            return bank
        ctx.enter_context(tc.manual_schedule())

        zeros = keep.tile([P, PAIR_COLS], BF16)
        nc.vector.memset(zeros[:], 0.0)
        bias_rows = keep.tile([P, P], BF16)
        nc.gpsimd.memset(bias_rows[:], 0.0)
        ident_f32 = keep.tile([P, P], F32)
        make_identity(nc, ident_f32[:])
        ident_bf16 = keep.tile([P, P], BF16)
        nc.vector.tensor_copy(out=ident_bf16[:], in_=ident_f32[:])

        idle_bank = psum_mx.tile([P, PAIR_COLS], F32, tag="mx")

        def keep_clock(passes):
            for turn in range(passes):
                nc.tensor.matmul(out=idle_bank[:], lhsT=zeros[:, 0:P], rhs=zeros[:], start=True, stop=True)

        x_sb = keep.tile([P, N_TILES * D_IN], BF16)
        h_sb = keep.tile([P, N_TILES * HID], BF16)
        s_sb = keep.tile([P, N_TILES * HID], BF16)
        c_sb = keep.tile([P, N_TILES, HID], BF16)
        w_in_sb = keep.tile([P, N_GATES * 2 * D_IN], BF16)
        w_rec_sb = keep.tile([P, N_GATES * 2 * HID], BF16)
        mask_sb = keep.tile([P, N_TILES], BF16)

        def load_batch(tile_sb, dram, first, count):
            view = tile_sb[:].rearrange("p (t n) -> p t n", t=N_TILES)
            nc.sync.dma_start(
                out=view[:, first : first + count, :],
                in_=by_batch_tile(dram)[:, first : first + count, :],
            )

        def load_gates(tile_sb, weights, first, gate, count=1):
            width = weights.shape[1]
            rows = weights[first * HID : (first + count) * HID, :]
            nc.sync.dma_start(
                out=tile_sb[:, gate * 2 * width : (gate + count) * 2 * width].rearrange(
                    "p (r n) -> p r n", n=width
                ),
                in_=rows.rearrange("(r p) n -> p r n", p=P),
            )

        def load_in_weights(gate, count=1):
            load_gates(w_in_sb, weight_ih, gate, gate, count)

        def as_rows(vector):
            return vector.rearrange("(r n) -> r n", n=P)

        rec_rows = N_RECURRENT * HID // P
        warm = keep.tile([P, 1], F32)
        nc.vector.memset(warm[:], 0.0)
        nc.scalar.activation(out=warm[:], in_=warm[:], func=ACT.Sigmoid)
        load_in_weights(0)
        load_batch(x_sb, x, 0, 2)
        load_in_weights(1)
        load_gates(w_rec_sb, weight_hh, 0, 0, 2)
        load_batch(h_sb, h_minors, 0, SIDE)
        nc.sync.dma_start(out=bias_rows[0:GATE_TILES, :], in_=as_rows(bias_ih))
        nc.sync.dma_start(out=bias_rows[GATE_TILES : GATE_TILES + rec_rows, :], in_=as_rows(bias_hh))
        nc.sync.dma_start(out=bias_rows[GATE_TILES + rec_rows : 2 * GATE_TILES, :], in_=as_rows(bias_sh))
        load_batch(x_sb, x, 2, 2)
        load_batch(x_sb, x, SIDE, SIDE)
        load_batch(h_sb, h_minors, SIDE, SIDE)
        load_in_weights(2)
        nc.sync.dma_start(out=mask_sb[:], in_=mask.rearrange("(p t) -> p t", t=N_TILES))
        nc.sync.dma_start(out=c_sb[:], in_=by_batch_tile(c_minors))
        load_in_weights(3)
        load_gates(w_rec_sb, weight_hh, 2, 2, 2)
        load_in_weights(4, 2)
        load_gates(w_rec_sb, weight_sh, 0, N_RECURRENT, 2)
        load_batch(s_sb, s_minors[idx, :, :], 0, N_TILES)

        bias_col = keep.tile([P, GATE_TILES], F32)

        def turn_biases():
            bias_turned = turn_bank([P, P], BF16)
            nc.tensor.transpose(bias_turned[:], bias_rows[:], ident_bf16[:])
            bias_parts = keep.tile([P, 2 * GATE_TILES], F32)
            nc.vector.tensor_copy(out=bias_parts[:], in_=bias_turned[:, 0 : 2 * GATE_TILES])
            nc.vector.tensor_tensor(
                out=bias_col[:], in0=bias_parts[:, 0:GATE_TILES], in1=bias_parts[:, GATE_TILES:], op=ALU.add
            )

        mask_f32 = keep.tile([P, N_TILES], F32)
        nc.gpsimd.tensor_copy(out=mask_f32[:], in_=mask_sb[:])

        x_codes = keep.tile([P, N_TILES * P], U32, align_bytes=64)
        x_scales = keep.tile([P, N_TILES * P], U8, align_bytes=64)
        w_codes = keep.tile([P, N_GATES * HID], U32, align_bytes=64)
        w_scales = keep.tile([P, N_GATES * HID], U8, align_bytes=64)
        h_T_words = keep.tile([P, N_TILES * P], F32)
        s_T_words = keep.tile([P, N_TILES * P], F32)
        w_rec_T_words = keep.tile([P, N_PAIRS * PAIR_COLS], F32)
        h_T = h_T_words[:].bitcast(BF16).rearrange("p (t b e) -> p t b e", t=N_TILES, e=2)
        s_T = s_T_words[:].bitcast(BF16).rearrange("p (t b e) -> p t b e", t=N_TILES, e=2)
        w_rec_T = w_rec_T_words[:].bitcast(BF16).rearrange("p (g n e) -> p g n e", g=N_PAIRS, e=2)

        def parted_words(source_sb, first_block):
            parted = stage.tile([P, 2, 2, P], F32)
            cols = slice(first_block * WORDS, (first_block + 2) * WORDS)
            nc.vector.tensor_copy(
                out=parted[:],
                in_=source_sb[:].bitcast(F32)[:, cols].rearrange("p (j w u) -> p j u w", j=2, u=2),
            )
            return parted

        def turn_parted(parted):
            turned = turn_bank([P, 2, 2, P], F32)
            for j in range(2):
                for u in range(2):
                    nc.tensor.transpose(turned[:, j, u, :], parted[:, j, u, :], ident_f32[:])
            return turned

        def turn_two_blocks(source_sb, first_block):
            words = source_sb[:].bitcast(F32)
            turned = turn_bank([P, 2, 2, P], F32)
            for j in range(2):
                for u in range(2):
                    first = (first_block + j) * WORDS + u
                    last = (first_block + j + 1) * WORDS
                    nc.tensor.transpose(turned[:, j, u, :], words[:, first:last:2], ident_f32[:])
            return turned

        def group_two_blocks(turned, copy_out):
            grouped = stage.tile([P, 2 * P * PACK], BF16, align_bytes=64)
            copy_out(
                out=grouped[:].bitcast(F32).rearrange("p (j r u) -> p j r u", j=2, u=2),
                in_=turned[:].rearrange("p j u r -> p j r u"),
            )
            return grouped

        def quantise_two_blocks(grouped, codes, scales, first_block):
            cols = slice(first_block * P, (first_block + 2) * P)
            nc.vector.quantize_mx(
                out=codes[:, cols].bitcast(FP8X4), scales=scales[:, cols], in_=grouped[:]
            )

        def turn_four_blocks(source_sb, first_block):
            words = source_sb[:].bitcast(F32)
            turned = turn_bank([P, SIDE * P], F32)
            for i in range(SIDE):
                cols = slice((first_block + i) * P, (first_block + i + 1) * P)
                nc.tensor.transpose(turned[:, i * P : (i + 1) * P], words[:, cols], ident_f32[:])
            return turned

        def copy_four_blocks(turned, dest_words, first_block, copy_out):
            copy_out(out=dest_words[:, first_block * P : (first_block + SIDE) * P], in_=turned[:])

        mx_T_of = {}

        def tiles_of_block(pair):
            return 2 if pair == 0 else SIDE

        def mx_bank(pair, first, gate_tiles):
            width = tiles_of_block(pair) * P
            batch = slice(first * P, first * P + width)
            bank = psum_mx.tile([P, PAIR_COLS], F32, tag="mx")
            for i, j in enumerate(gate_tiles):
                rows = slice((SIDE * pair + j) * P, (SIDE * pair + j + 1) * P)
                nc.tensor.matmul_mx(
                    out=bank[:, i * width : (i + 1) * width],
                    lhsT=w_codes[:, rows].bitcast(FP8X4),
                    lhsT_scale=w_scales[:, rows],
                    rhs=x_codes[:, batch].bitcast(FP8X4),
                    rhs_scale=x_scales[:, batch],
                    start=True,
                    stop=True,
                )
            return bank

        def mx_out(pair, first, gate_tiles, bank, on_scalar):
            width = tiles_of_block(pair) * P
            if gate_tiles[0] == 0:
                mx_T_block = mx_pool.tile([P, SIDE, SIDE * P], F32)
                mx_T_of[(pair, first)] = mx_T_block
            mx_T = mx_T_of[(pair, first)]
            for i, j in enumerate(gate_tiles):
                bias = bias_col[:, SIDE * pair + j : SIDE * pair + j + 1]
                product = bank[:, i * width : (i + 1) * width]
                if on_scalar:
                    nc.scalar.activation(out=mx_T[:, j, 0:width], in_=product, func=ACT.Identity, bias=bias)
                else:
                    nc.vector.tensor_scalar_add(out=mx_T[:, j, 0:width], in0=product, scalar1=bias)

        steps = [(0, t) for t in range(N_TILES)]
        for t in range(N_TILES + SHARE_LAG):
            if t < N_TILES:
                steps.append((1, t))
            if t >= SHARE_LAG:
                steps.append((2, t - SHARE_LAG))
        pre_of = {}
        gates = keep.tile([P, N_PAIRS, N_TILES, PAIR_COLS], F32)

        def plain_pass(pair, t, c):
            if c == 0:
                bank = psum_pre.tile([P, PAIR_COLS], F32, tag="pre")
                pre_of[(pair, t)] = bank
            state_T = h_T if 2 * pair < N_RECURRENT else s_T
            nc.tensor.matmul(
                out=pre_of[(pair, t)][:],
                lhsT=state_T[:, t, :, c],
                rhs=w_rec_T[:, pair, :, c],
                start=(c == 0),
                stop=False,
            )

        def add_mx_product(pair, t, j):
            tiles = tiles_of_block(pair)
            q = t % tiles
            nc.tensor.matmul(
                out=pre_of[(pair, t)][:, j * P : (j + 1) * P],
                lhsT=mx_T_of[(pair, t - q)][:, j, q * P : (q + 1) * P],
                rhs=ident_f32[:],
                is_transpose=True,
                start=False,
                stop=(j == SIDE - 1),
            )

        def is_last(pair, t):
            return (pair, t) == steps[-1]

        def activations(pair, t):
            pre = pre_of[(pair, t)]
            if pair == 1:
                nc.scalar.activation(out=gates[:, pair, t, 0:HID], in_=pre[:, 0:HID], func=ACT.Sigmoid)
                nc.scalar.activation(out=gates[:, pair, t, HID:], in_=pre[:, HID:], func=ACT.Tanh)
            elif is_last(pair, t):
                for share in range(2):
                    cols = slice(share * HID, (share + 1) * HID)
                    nc.scalar.activation(out=gates[:, pair, t, cols], in_=pre[:, cols], func=ACT.Sigmoid)
            else:
                nc.scalar.activation(out=gates[:, pair, t, :], in_=pre[:], func=ACT.Sigmoid)

        masked_c = keep.tile([P, N_TILES, HID], F32)
        kept = keep.tile([P, N_TILES, HID], F32)
        squashed = keep.tile([P, N_TILES, HID], F32)
        h_res = keep.tile([P, N_TILES, HID], F32)
        c_res = keep.tile([P, N_TILES, HID], F32)
        s_res = keep.tile([P, 2, N_TILES, HID], F32)

        def store(dram, result, t):
            nc.sync.dma_start(out=by_batch_tile(dram)[:, t, :], in_=result[:, t, :])

        def masked_product(out, in0, in1, t):
            nc.vector.scalar_tensor_tensor(
                out=out, in0=in0, scalar=mask_f32[:, t : t + 1], in1=in1, op0=ALU.mult, op1=ALU.mult
            )

        in_term_of = {}

        def products(pair, t):
            if pair == 0:
                nc.gpsimd.tensor_scalar(
                    out=masked_c[:, t, :],
                    in0=c_sb[:, t, :],
                    scalar1=mask_f32[:, t : t + 1],
                    scalar2=0.0,
                    op0=ALU.mult,
                    op1=ALU.add,
                )
                nc.gpsimd.tensor_tensor(
                    out=kept[:, t, :], in0=gates[:, 0, t, HID:], in1=masked_c[:, t, :], op=ALU.mult
                )
            elif pair == 1:
                in_term = stage.tile([P, HID], F32)
                in_term_of[t] = in_term
                masked_product(in_term[:], gates[:, 0, t, 0:HID], gates[:, 1, t, HID:], t)
            else:
                for shares in [slice(0, 1), slice(1, 2)] if is_last(pair, t) else [slice(0, 2)]:
                    count = shares.stop - shares.start
                    masked_product(
                        s_res[:, shares, t, :],
                        squashed[:, t, :].unsqueeze(1).to_broadcast([P, count, HID]),
                        gates[:, 2, t, :].rearrange("p (s n) -> p s n", s=2)[:, shares, :],
                        t,
                    )
                    for share in range(shares.start, shares.stop):
                        store((out_s0, out_s1)[share], s_res[:, share, :, :], t)

        def new_cell(pair, t):
            if pair == 1:
                nc.vector.tensor_tensor(
                    out=c_res[:, t, :], in0=in_term_of[t][:], in1=kept[:, t, :], op=ALU.add
                )
                store(out_c, c_res, t)

        def squash(pair, t):
            if pair == 1:
                nc.scalar.activation(out=squashed[:, t, :], in_=c_res[:, t, :], func=ACT.Tanh)

        def new_hidden(pair, t):
            if pair == 1:
                masked_product(h_res[:, t, :], squashed[:, t, :], gates[:, 1, t, 0:HID], t)
                store(out_h, h_res, t)

        keep_clock(3)
        w_turned = turn_two_blocks(w_in_sb, 0)
        keep_clock(1)
        first_w = group_two_blocks(w_turned, nc.vector.tensor_copy)
        x_turned = turn_two_blocks(x_sb, 0)
        keep_clock(1)
        first_x = group_two_blocks(x_turned, nc.scalar.copy)
        quantise_two_blocks(first_w, w_codes, w_scales, 0)
        w_turned = turn_two_blocks(w_in_sb, 2)
        keep_clock(1)
        second_w = group_two_blocks(w_turned, nc.scalar.copy)
        quantise_two_blocks(first_x, x_codes, x_scales, 0)
        rec_turned = turn_four_blocks(w_rec_sb, 0)
        keep_clock(1)
        h_turned = turn_four_blocks(h_sb, 0)
        keep_clock(1)
        quantise_two_blocks(second_w, w_codes, w_scales, 2)
        copy_four_blocks(rec_turned, w_rec_T_words, 0, nc.vector.tensor_copy)
        copy_four_blocks(h_turned, h_T_words, 0, nc.scalar.copy)
        x_turned = turn_two_blocks(x_sb, 2)
        second_x = group_two_blocks(x_turned, nc.vector.tensor_copy)

        mx_at = {}
        for n, (pair, t) in enumerate(steps):
            if t % tiles_of_block(pair) == 0:
                fills = [(0, 1), (2, 3)] if pair == 0 else [(j,) for j in range(SIDE)]
                for i, gate_tiles in enumerate(fills):
                    mx_at.setdefault(n - 1 - len(fills) + i, []).append((pair, t, gate_tiles))

        def quantised(source_sb, first, codes, scales, copy_out):
            made = []
            return [
                lambda: made.append(turn_two_blocks(source_sb, first)),
                lambda: made.append(group_two_blocks(made[0], copy_out)),
                lambda: quantise_two_blocks(made[1], codes, scales, first),
            ]

        def parted_and_quantised(source_sb, first, codes, scales, copy_out):
            made = []
            return [
                lambda: made.append(parted_words(source_sb, first)),
                lambda: made.append(turn_parted(made[0])),
                lambda: made.append(group_two_blocks(made[1], copy_out)),
                lambda: quantise_two_blocks(made[2], codes, scales, first),
            ]

        def turned_words(source_sb, first, dest_words, copy_out):
            made = []
            return [
                lambda: made.append(turn_four_blocks(source_sb, first)),
                lambda: copy_four_blocks(made[0], dest_words, first, copy_out),
            ]

        on_vector = nc.vector.tensor_copy
        on_scalar = nc.scalar.copy
        jobs = [
            (-2, quantised(x_sb, 4, x_codes, x_scales, on_vector)),
            (-1, quantised(w_in_sb, 4, w_codes, w_scales, on_vector)),
            (0, quantised(x_sb, 6, x_codes, x_scales, on_scalar)),
            (1, turned_words(h_sb, SIDE, h_T_words, on_vector)),
            (2, parted_and_quantised(w_in_sb, 6, w_codes, w_scales, on_vector)),
            (4, turned_words(w_rec_sb, SIDE, w_rec_T_words, on_scalar)),
            (5, parted_and_quantised(w_in_sb, 8, w_codes, w_scales, on_vector)),
            (7, parted_and_quantised(w_in_sb, 10, w_codes, w_scales, on_vector)),
            (9, turned_words(w_rec_sb, 2 * SIDE, w_rec_T_words, on_vector)),
            (10, turned_words(s_sb, 0, s_T_words, on_vector)),
            (14, turned_words(s_sb, SIDE, s_T_words, on_scalar)),
        ]
        parts_at = {}
        parts_at[-2] = [(2, lambda: quantise_two_blocks(second_x, x_codes, x_scales, 2))]
        for start, parts in jobs:
            for i, part in enumerate(parts, -1 if len(parts) == 4 else 0):
                parts_at.setdefault(start + i, []).append((i, part))

        def do_parts(n, number):
            for i, part in parts_at.get(n, []):
                if i == number:
                    part()

        def lagged(stage_of_step, n, lag):
            if 0 <= n - lag < len(steps):
                stage_of_step(*steps[n - lag])

        head[0] = False
        full_banks = []
        turns = 0
        for n in range(-3, len(steps) + 5):
            coming = n + AHEAD
            filled = []
            if 0 <= coming < len(steps):
                plain_pass(*steps[coming], 0)
            for fill in mx_at.get(n, []):
                filled.append((*fill, mx_bank(*fill)))
            if n == -3:
                turn_biases()
            if 0 <= coming < len(steps):
                plain_pass(*steps[coming], 1)
            if 0 <= n < len(steps):
                for j in range(SIDE):
                    add_mx_product(*steps[n], j)
            lagged(activations, n, 1)
            for full in full_banks:
                mx_out(*full, turns % 2 == 0)
                turns += 1
            full_banks = filled
            lagged(products, n, 2)
            lagged(new_cell, n, 3)
            do_parts(n, 1)
            do_parts(n, 2)
            do_parts(n, 0)
            do_parts(n, -1)
            lagged(squash, n, 4)
            lagged(new_hidden, n, 5)
